import numpy as np
import ml_dtypes


def mxq(x, axis, fmt="e4m3"):
    dtype, down = {"e4m3": (ml_dtypes.float8_e4m3fn, 7), "e5m2": (ml_dtypes.float8_e5m2, 14)}[fmt]
    v = np.moveaxis(np.asarray(x, np.float32).astype(ml_dtypes.bfloat16).astype(np.float64), axis, -1)
    blocks = v.reshape(v.shape[:-1] + (-1, 32))
    amax = np.abs(blocks).max(-1, keepdims=True)
    byte = np.maximum(np.where(amax > 0, np.frexp(amax)[1] - 1 + 127, 0) - down, 1)
    scale = np.exp2(byte - 127.0)
    codes = (blocks / scale).astype(np.float32).astype(dtype).astype(np.float64)
    return np.moveaxis((codes * scale).reshape(v.shape), -1, axis)


WIDE = False


def mx_kscale(k):
    if not WIDE:
        return np.ones(k)
    levels = np.array([10, -10, 5, -5, 0])
    if k % 512:
        return np.exp2(np.random.permutation(np.resize(levels, k // 32))).repeat(32)
    a = np.empty((k // 512, 16))
    for p in range(k // 512):
        a[p, :8] = np.random.permutation(np.resize(levels, 8))
        for g in range(8):
            far = levels[np.abs(levels - a[p, g]) >= 10]
            a[p, g + 8] = far[np.random.randint(len(far))]
    return np.exp2(a.ravel()).repeat(32)


BF16 = ml_dtypes.bfloat16


def bf(x):
    return np.asarray(x, np.float32).astype(BF16)


def f64(x):
    return np.asarray(x).astype(np.float64)


T, B, D, H, HD, A = 512, 8, 512, 4, 128, 128
HH = H * HD
CAT = HH + D
EPS = 1e-5
AO = 0.6


def layer_norm(x, w, b):
    mu = x.mean(-1, keepdims=True)
    var = np.square(x - mu).mean(-1, keepdims=True)
    return (x - mu) * (1.0 / np.sqrt(var + EPS)) * w + b


def setup_inputs():
    t = mx_kscale(HH)
    w_out = np.random.standard_normal((CAT, D)) / np.sqrt(CAT)
    w_out[:HH] = w_out[:HH] / t[:, None]
    return {"u": bf(np.random.standard_normal((T, B, HH)) * t),
            "attn_out": bf(AO * np.random.standard_normal((T, B, HH)) * t),
            "src_norm": bf(np.random.standard_normal((T, B, D))),
            "w_out": bf(w_out),
            "b_out": bf(0.1 * np.random.standard_normal(D)),
            "ln2_w": bf(1.0 + 0.1 * np.random.standard_normal(D)),
            "ln2_b": bf(0.1 * np.random.standard_normal(D))}


def reference(u, attn_out, src_norm, w_out, b_out, ln2_w, ln2_b):
    residual = f64(u) + f64(attn_out)
    xn = f64(src_norm)
    cat = np.concatenate([residual, xn], -1)
    z = (mxq(cat, 2, "e4m3") @ mxq(f64(w_out), 0, "e4m3")) + f64(b_out)
    return layer_norm(z, f64(ln2_w), f64(ln2_b)) + xn

@@ -1,0 +1,261 @@
+from contextlib import ExitStack
+
+import concourse.mybir as mybir
+from concourse.masks import make_identity
+
+F32 = mybir.dt.float32
+BF16 = mybir.dt.bfloat16
+U32 = mybir.dt.uint32
+U8 = mybir.dt.uint8
+FP8X4 = mybir.dt.float8_e4m3fn_x4
+ALU = mybir.AluOpType
+ACT = mybir.ActivationFunctionType
+
+P = 128
+ROWS = 512 * 8
+D = 512
+BLOCKS = D // P
+PASSES = 2
+HALVES = 2
+TILES = ROWS // P
+PAIR = 2
+PAIR_ROWS = PAIR * P
+PAIRS = ROWS // PAIR_ROWS
+EPS = 1e-5
+ROUNDS_BEFORE_QUANTISING_WEIGHT = 2
+LAST_LAG = 13
+
+FLOPS = 2 * ROWS * (PASSES * 512) * D
+
+
+def tile_stulayer_pb_t_kernel(tc, u, attn_out, src_norm, w_out, b_out, ln2_w, ln2_b, out):
+    nc = tc.nc
+
+    def pair_rows(x, j):
+        rows = x.flatten_outer_dims()[j * PAIR_ROWS : (j + 1) * PAIR_ROWS, :]
+        return rows.rearrange("(p i) d -> p (i d)", i=PAIR)
+
+    def tile_rows(x, m):
+        j, i = divmod(m, PAIR)
+        return pair_rows(x, j)[:, i * D : (i + 1) * D]
+
+    with ExitStack() as pools:
+        const = pools.enter_context(tc.tile_pool(name="const", bufs=1))
+        inputs = pools.enter_context(tc.tile_pool(name="inputs", bufs=1))
+        two = pools.enter_context(tc.tile_pool(name="two", bufs=2))
+        three = pools.enter_context(tc.tile_pool(name="three", bufs=3))
+        four = pools.enter_context(tc.tile_pool(name="four", bufs=4))
+        six = pools.enter_context(tc.tile_pool(name="six", bufs=6))
+        psum = pools.enter_context(tc.psum_pool(name="psum", bufs=2))
+
+        vec_rows = const.tile([P, P], BF16)
+        nc.vector.memset(vec_rows[:], 0.0)
+        nc.scalar.dma_start(out=vec_rows[0:BLOCKS, :], in_=ln2_w.rearrange("(f p) -> f p", p=P))
+        nc.scalar.dma_start(out=vec_rows[BLOCKS : 2 * BLOCKS, :], in_=ln2_b.rearrange("(f p) -> f p", p=P))
+        b_row = const.tile([P, D], BF16)
+        nc.vector.memset(b_row[:], 0.0)
+        nc.scalar.dma_start(out=b_row[0:1, :], in_=b_out.rearrange("(o d) -> o d", o=1))
+        w_raw = const.tile([P, PASSES, 4 * D], BF16)
+        nc.sync.dma_start(
+            out=w_raw[:],
+            in_=w_out.rearrange("(c q t) n -> q c (t n)", c=PASSES, t=4),
+        )
+
+        u_sb, a_sb, x_sb = [], [], []
+        for j in range(PAIRS):
+            u_j = inputs.tile([P, PAIR * D], BF16, name="u%d" % j)
+            a_j = inputs.tile([P, PAIR * D], BF16, name="a%d" % j)
+            x_j = inputs.tile([P, PAIR * D], BF16, name="x%d" % j)
+            nc.sync.dma_start(out=u_j[:], in_=pair_rows(u, j))
+            nc.sync.dma_start(out=a_j[:], in_=pair_rows(attn_out, j))
+            nc.sync.dma_start(out=x_j[:], in_=pair_rows(src_norm, j))
+            u_sb.append(u_j)
+            a_sb.append(a_j)
+            x_sb.append(x_j)
+
+        ident = const.tile([P, P], F32)
+        make_identity(nc, ident[:])
+        ones = const.tile([P, P], BF16)
+        nc.vector.memset(ones[:], 1.0)
+        eps_col = const.tile([P, 1], F32)
+        nc.vector.memset(eps_col[:], EPS)
+        first_sqrt = const.tile([P, 1], F32)
+        nc.scalar.activation(out=first_sqrt[:], in_=eps_col[:], func=ACT.Sqrt)
+
+        w_grouped = const.tile([P, PASSES, D * 4], BF16, align_bytes=64)
+        w_codes = const.tile([P, PASSES, D], U32, align_bytes=64)
+        w_scales = const.tile([P, PASSES, D], U8, align_bytes=64)
+        vec_rows_f32 = const.tile([P, P], F32)
+        vec_cols = const.tile([P, 2 * BLOCKS], F32)
+        b_bc = const.tile([P, D], F32)
+
+        def regroup_weight():
+            for c in range(PASSES):
+                rows_of_pass = w_raw[:, c, :].rearrange("p (t n) -> p n t", t=4)
+                words_of_pass = w_grouped[:, c, :].rearrange("p (n t) -> p n t", t=4)
+                if c == 0:
+                    nc.vector.tensor_copy(out=words_of_pass, in_=rows_of_pass)
+                else:
+                    nc.scalar.copy(out=words_of_pass, in_=rows_of_pass)
+
+        def quantise_weight():
+            for c in range(PASSES):
+                nc.vector.quantize_mx(
+                    out=w_codes[:, c, :].bitcast(FP8X4), scales=w_scales[:, c, :], in_=w_grouped[:, c, :]
+                )
+
+        def prepare_gain_shift():
+            nc.vector.tensor_copy(out=vec_rows_f32[:], in_=vec_rows[:])
+            vec_t = psum.tile([P, D], F32, tag="w_ps")
+            nc.tensor.transpose(vec_t[:, 0:P], vec_rows_f32[:], ident[:])
+            nc.vector.tensor_copy(out=vec_cols[:], in_=vec_t[:, 0 : 2 * BLOCKS])
+
+        def prepare_bias():
+            b_ps = psum.tile([P, D], F32, tag="y_t")
+            nc.tensor.matmul(out=b_ps[:], lhsT=ones[:], rhs=b_row[:], start=True, stop=True)
+            nc.vector.tensor_copy(out=b_bc[:], in_=b_ps[:])
+
+        res, cat_t, grouped, codes, scales, z, zb, y, y_t, w_t, w_ps, result = {}, {}, {}, {}, {}, {}, {}, {}, {}, {}, {}, {}
+        row_sum, neg_mean, sq_sum, std, rstd = {}, {}, {}, {}, {}
+
+        def add_inputs(m):
+            j, i = divmod(m, PAIR)
+            cols = slice(i * D, (i + 1) * D)
+            res[m] = three.tile([P, D], BF16, name="res")
+            nc.vector.tensor_tensor(out=res[m][:], in0=u_sb[j][:, cols], in1=a_sb[j][:, cols], op=ALU.add)
+
+        def transpose_cat(m):
+            j, i = divmod(m, PAIR)
+            cat_words = [res[m][:].bitcast(F32), x_sb[j][:].bitcast(F32)[:, i * (D // 2) : (i + 1) * (D // 2)]]
+            cat_t[m] = psum.tile([P, PASSES * HALVES, P], F32, tag="cat_t", name="cat_t")
+            for c in range(PASSES):
+                for h in range(HALVES):
+                    nc.tensor.transpose(
+                        cat_t[m][:, c * HALVES + h, :], cat_words[c][:, h : HALVES * P : HALVES], ident[:]
+                    )
+
+        def copy_cat(m):
+            grouped[m] = three.tile([P, PASSES * P * 4], BF16, align_bytes=64, name="grouped")
+            nc.scalar.copy(
+                out=grouped[m][:].bitcast(F32).rearrange("p (c r h) -> p c r h", c=PASSES, h=HALVES),
+                in_=cat_t[m][:].rearrange("p (c h) r -> p c r h", h=HALVES),
+            )
+
+        def quantise(m):
+            codes[m] = three.tile([P, PASSES * P], U32, align_bytes=64, name="codes")
+            scales[m] = three.tile([P, PASSES * P], U8, align_bytes=64, name="scales")
+            nc.vector.quantize_mx(out=codes[m][:].bitcast(FP8X4), scales=scales[m][:], in_=grouped[m][:])
+
+        def project(m):
+            z[m] = psum.tile([P, D], F32, tag="z", name="z")
+            for c in range(PASSES):
+                cols = slice(c * P, (c + 1) * P)
+                nc.tensor.matmul_mx(
+                    out=z[m][:],
+                    lhsT=codes[m][:, cols].bitcast(FP8X4),
+                    lhsT_scale=scales[m][:, cols],
+                    rhs=w_codes[:, c, :].bitcast(FP8X4),
+                    rhs_scale=w_scales[:, c, :],
+                    start=(c == 0),
+                    stop=(c == PASSES - 1),
+                )
+
+        def add_bias(m):
+            zb[m] = four.tile([P, D], F32, name="zb")
+            row_sum[m] = four.tile([P, 1], F32, name="row_sum")
+            nc.vector.scalar_tensor_tensor(
+                out=zb[m][:], in0=z[m][:], scalar=1.0, in1=b_bc[:], op0=ALU.mult, op1=ALU.add,
+                accum_out=row_sum[m][:],
+            )
+
+        def minus_mean(m):
+            neg_mean[m] = four.tile([P, 1], F32, name="neg_mean")
+            nc.gpsimd.tensor_scalar(
+                out=neg_mean[m][:], in0=row_sum[m][:], scalar1=-1.0 / D, scalar2=0.0, op0=ALU.mult, op1=ALU.add
+            )
+
+        def square_sum(m):
+            squares = two.tile([P, D], BF16, name="squares")
+            sq_sum[m] = four.tile([P, 1], F32, name="sq_sum")
+            nc.scalar.activation(
+                out=squares[:], in_=zb[m][:], func=ACT.Square, bias=neg_mean[m][:], scale=1.0, accum_out=sq_sum[m][:]
+            )
+
+        def standard_deviation(m):
+            std[m] = four.tile([P, 1], F32, name="std")
+            nc.scalar.activation(out=std[m][:], in_=sq_sum[m][:], func=ACT.Sqrt, bias=eps_col[:], scale=1.0 / D)
+
+        def invert_std(m):
+            rstd[m] = four.tile([P, 1], F32, name="rstd")
+            nc.vector.reciprocal(out=rstd[m][:], in_=std[m][:])
+
+        def normalise(m):
+            y[m] = six.tile([P, D], F32, name="y")
+            nc.gpsimd.tensor_scalar(
+                out=y[m][:], in0=zb[m][:], scalar1=neg_mean[m][:], scalar2=rstd[m][:], op0=ALU.add, op1=ALU.mult
+            )
+
+        def blocks_of(bank):
+            return range(bank * (BLOCKS // PAIR), (bank + 1) * (BLOCKS // PAIR))
+
+        def transpose_y(s):
+            j, bank = divmod(s, PAIR)
+            y_t[s] = psum.tile([P, BLOCKS // PAIR, PAIR, P], F32, tag="y_t", name="y_t")
+            for slot, f in enumerate(blocks_of(bank)):
+                for i in range(PAIR):
+                    nc.tensor.transpose(y_t[s][:, slot, i, :], y[j * PAIR + i][:, f * P : (f + 1) * P], ident[:])
+
+        def gain_shift(s):
+            j, bank = divmod(s, PAIR)
+            if bank == 0:
+                w_t[j] = three.tile([P, BLOCKS, PAIR, P], F32, name="w_t")
+            for slot, f in enumerate(blocks_of(bank)):
+                nc.scalar.activation(
+                    out=w_t[j][:, f, :, :], in_=y_t[s][:, slot, :, :], func=ACT.Identity,
+                    scale=vec_cols[:, f : f + 1], bias=vec_cols[:, BLOCKS + f : BLOCKS + f + 1],
+                )
+
+        def transpose_back(m):
+            j, i = divmod(m, PAIR)
+            w_ps[m] = psum.tile([P, D], F32, tag="w_ps", name="w_ps")
+            for f in range(BLOCKS):
+                nc.tensor.transpose(w_ps[m][:, f * P : (f + 1) * P], w_t[j][:, f, i, :], ident[:])
+
+        def add_src(m):
+            j, i = divmod(m, PAIR)
+            result[m] = four.tile([P, D], F32, name="result")
+            nc.vector.tensor_tensor(
+                out=result[m][:], in0=w_ps[m][:], in1=x_sb[j][:, i * D : (i + 1) * D], op=ALU.add
+            )
+            nc.sync.dma_start(out=tile_rows(out, m), in_=result[m][:])
+
+        def run(stage, m):
+            if 0 <= m < TILES:
+                stage(m)
+
+        def one_round(h):
+            run(quantise, h - 3)
+            run(add_inputs, h)
+            run(invert_std, h - 7)
+            run(normalise, h - 7)
+            run(add_bias, h - 5)
+            run(minus_mean, h - 5)
+            run(add_src, h - 13)
+            run(copy_cat, h - 2)
+            run(square_sum, h - 6)
+            run(gain_shift, h - 10)
+            run(standard_deviation, h - 6)
+            run(transpose_back, h - 12)
+            run(transpose_y, h - 9)
+            run(transpose_cat, h - 1)
+            run(project, h - 4)
+
+        with tc.manual_schedule():
+            regroup_weight()
+            for h in range(ROUNDS_BEFORE_QUANTISING_WEIGHT):
+                one_round(h)
+            quantise_weight()
+            prepare_bias()
+            prepare_gain_shift()
+            for h in range(ROUNDS_BEFORE_QUANTISING_WEIGHT, TILES + LAST_LAG + 1):
+                one_round(h)

@@ -78,9 +78,9 @@ def tile_stulayer_pb_t_kernel(tc, u, attn_out, src_norm, w_out, b_out, ln2_w, ln
         ones = const.tile([P, P], BF16)
         nc.vector.memset(ones[:], 1.0)
         eps_col = const.tile([P, 1], F32)
-        nc.vector.memset(eps_col[:], EPS)
-        first_sqrt = const.tile([P, 1], F32)
-        nc.scalar.activation(out=first_sqrt[:], in_=eps_col[:], func=ACT.Sqrt)
+        nc.vector.memset(eps_col[:], EPS / D**2)
+        first_rsqrt = const.tile([P, 1], F32)
+        nc.scalar.activation(out=first_rsqrt[:], in_=eps_col[:], func=ACT.Abs_reciprocal_sqrt)
 
         w_grouped = const.tile([P, PASSES, D * 4], BF16, align_bytes=64)
         w_codes = const.tile([P, PASSES, D], U32, align_bytes=64)
@@ -113,10 +113,12 @@ def tile_stulayer_pb_t_kernel(tc, u, attn_out, src_norm, w_out, b_out, ln2_w, ln
         def prepare_bias():
             b_ps = psum.tile([P, D], F32, tag="y_t")
             nc.tensor.matmul(out=b_ps[:], lhsT=ones[:], rhs=b_row[:], start=True, stop=True)
-            nc.vector.tensor_copy(out=b_bc[:], in_=b_ps[:])
+            nc.vector.tensor_scalar(
+                out=b_bc[:], in0=b_ps[:], scalar1=1.0 / D, scalar2=0.0, op0=ALU.mult, op1=ALU.add
+            )
 
         res, cat_t, grouped, codes, scales, z, zb, y, y_t, w_t, w_ps, result = {}, {}, {}, {}, {}, {}, {}, {}, {}, {}, {}, {}
-        row_sum, neg_mean, sq_sum, std, rstd = {}, {}, {}, {}, {}
+        mean, neg_mean, sq_sum, rstd = {}, {}, {}, {}
 
         def add_inputs(m):
             j, i = divmod(m, PAIR)
@@ -162,32 +164,31 @@ def tile_stulayer_pb_t_kernel(tc, u, attn_out, src_norm, w_out, b_out, ln2_w, ln
 
         def add_bias(m):
             zb[m] = four.tile([P, D], F32, name="zb")
-            row_sum[m] = four.tile([P, 1], F32, name="row_sum")
+            mean[m] = four.tile([P, 1], F32, name="mean")
             nc.vector.scalar_tensor_tensor(
-                out=zb[m][:], in0=z[m][:], scalar=1.0, in1=b_bc[:], op0=ALU.mult, op1=ALU.add,
-                accum_out=row_sum[m][:],
+                out=zb[m][:], in0=z[m][:], scalar=1.0 / D, in1=b_bc[:], op0=ALU.mult, op1=ALU.add,
+                accum_out=mean[m][:],
             )
 
-        def minus_mean(m):
+        def mean_over_d(m):
             neg_mean[m] = four.tile([P, 1], F32, name="neg_mean")
             nc.gpsimd.tensor_scalar(
-                out=neg_mean[m][:], in0=row_sum[m][:], scalar1=-1.0 / D, scalar2=0.0, op0=ALU.mult, op1=ALU.add
+                out=neg_mean[m][:], in0=mean[m][:], scalar1=-1.0 / D, scalar2=0.0, op0=ALU.mult, op1=ALU.add
             )
 
         def square_sum(m):
             squares = two.tile([P, D], BF16, name="squares")
             sq_sum[m] = four.tile([P, 1], F32, name="sq_sum")
             nc.scalar.activation(
-                out=squares[:], in_=zb[m][:], func=ACT.Square, bias=neg_mean[m][:], scale=1.0, accum_out=sq_sum[m][:]
+                out=squares[:], in_=zb[m][:], func=ACT.Square, bias=mean[m][:], scale=float(-D),
+                accum_out=sq_sum[m][:],
             )
 
-        def standard_deviation(m):
-            std[m] = four.tile([P, 1], F32, name="std")
-            nc.scalar.activation(out=std[m][:], in_=sq_sum[m][:], func=ACT.Sqrt, bias=eps_col[:], scale=1.0 / D)
-
-        def invert_std(m):
+        def inverse_deviation(m):
             rstd[m] = four.tile([P, 1], F32, name="rstd")
-            nc.vector.reciprocal(out=rstd[m][:], in_=std[m][:])
+            nc.scalar.activation(
+                out=rstd[m][:], in_=sq_sum[m][:], func=ACT.Abs_reciprocal_sqrt, bias=eps_col[:], scale=1.0 / D**3
+            )
 
         def normalise(m):
             y[m] = six.tile([P, D], F32, name="y")
@@ -236,15 +237,14 @@ def tile_stulayer_pb_t_kernel(tc, u, attn_out, src_norm, w_out, b_out, ln2_w, ln
         def one_round(h):
             run(quantise, h - 3)
             run(add_inputs, h)
-            run(invert_std, h - 7)
             run(normalise, h - 7)
             run(add_bias, h - 5)
-            run(minus_mean, h - 5)
+            run(mean_over_d, h - 5)
             run(add_src, h - 13)
             run(copy_cat, h - 2)
             run(square_sum, h - 6)
             run(gain_shift, h - 10)
-            run(standard_deviation, h - 6)
+            run(inverse_deviation, h - 6)
             run(transpose_back, h - 12)
             run(transpose_y, h - 9)
             run(transpose_cat, h - 1)

@@ -23,6 +23,8 @@ PAIR_ROWS = PAIR * P
 PAIRS = ROWS // PAIR_ROWS
 EPS = 1e-5
 ROUNDS_BEFORE_QUANTISING_WEIGHT = 2
+QUANT_LAG = 3
+NORM_LAG = 7
 LAST_LAG = 13
 
 FLOPS = 2 * ROWS * (PASSES * 512) * D
@@ -45,7 +47,7 @@ def tile_stulayer_pb_t_kernel(tc, u, attn_out, src_norm, w_out, b_out, ln2_w, ln
         two = pools.enter_context(tc.tile_pool(name="two", bufs=2))
         three = pools.enter_context(tc.tile_pool(name="three", bufs=3))
         four = pools.enter_context(tc.tile_pool(name="four", bufs=4))
-        six = pools.enter_context(tc.tile_pool(name="six", bufs=6))
+        seven = pools.enter_context(tc.tile_pool(name="seven", bufs=7))
         psum = pools.enter_context(tc.psum_pool(name="psum", bufs=2))
 
         vec_rows = const.tile([P, P], BF16)
@@ -137,7 +139,7 @@ def tile_stulayer_pb_t_kernel(tc, u, attn_out, src_norm, w_out, b_out, ln2_w, ln
                     )
 
         def copy_cat(m):
-            grouped[m] = three.tile([P, PASSES * P * 4], BF16, align_bytes=64, name="grouped")
+            grouped[m] = seven.tile([P, PASSES * P * 4], BF16, align_bytes=64, name="grouped")
             nc.scalar.copy(
                 out=grouped[m][:].bitcast(F32).rearrange("p (c r h) -> p c r h", c=PASSES, h=HALVES),
                 in_=cat_t[m][:].rearrange("p (c h) r -> p c r h", h=HALVES),
@@ -191,9 +193,11 @@ def tile_stulayer_pb_t_kernel(tc, u, attn_out, src_norm, w_out, b_out, ln2_w, ln
             )
 
         def normalise(m):
-            y[m] = six.tile([P, D], F32, name="y")
+            k = m + NORM_LAG - QUANT_LAG
+            y_tile = grouped[k] if k < TILES else seven.tile([P, PASSES * P * 4], BF16, align_bytes=64, name="grouped")
+            y[m] = y_tile[:].bitcast(F32)
             nc.gpsimd.tensor_scalar(
-                out=y[m][:], in0=zb[m][:], scalar1=neg_mean[m][:], scalar2=rstd[m][:], op0=ALU.add, op1=ALU.mult
+                out=y[m], in0=zb[m][:], scalar1=neg_mean[m][:], scalar2=rstd[m][:], op0=ALU.add, op1=ALU.mult
             )
 
         def blocks_of(bank):
@@ -235,9 +239,9 @@ def tile_stulayer_pb_t_kernel(tc, u, attn_out, src_norm, w_out, b_out, ln2_w, ln
                 stage(m)
 
         def one_round(h):
-            run(quantise, h - 3)
             run(add_inputs, h)
-            run(normalise, h - 7)
+            run(quantise, h - QUANT_LAG)
+            run(normalise, h - NORM_LAG)
             run(add_bias, h - 5)
             run(mean_over_d, h - 5)
             run(add_src, h - 13)

@@ -22,7 +22,6 @@ PAIR = 2
 PAIR_ROWS = PAIR * P
 PAIRS = ROWS // PAIR_ROWS
 EPS = 1e-5
-ROUNDS_BEFORE_QUANTISING_WEIGHT = 2
 QUANT_LAG = 3
 NORM_LAG = 7
 LAST_LAG = 13
@@ -50,21 +49,19 @@ def tile_stulayer_pb_t_kernel(tc, u, attn_out, src_norm, w_out, b_out, ln2_w, ln
         seven = pools.enter_context(tc.tile_pool(name="seven", bufs=7))
         psum = pools.enter_context(tc.psum_pool(name="psum", bufs=2))
 
+        b_row = const.tile([P, D], BF16)
+        nc.vector.memset(b_row[:], 0.0)
+        nc.scalar.dma_start(out=b_row[0:1, :], in_=b_out.rearrange("(o d) -> o d", o=1))
         vec_rows = const.tile([P, P], BF16)
         nc.vector.memset(vec_rows[:], 0.0)
         nc.scalar.dma_start(out=vec_rows[0:BLOCKS, :], in_=ln2_w.rearrange("(f p) -> f p", p=P))
         nc.scalar.dma_start(out=vec_rows[BLOCKS : 2 * BLOCKS, :], in_=ln2_b.rearrange("(f p) -> f p", p=P))
-        b_row = const.tile([P, D], BF16)
-        nc.vector.memset(b_row[:], 0.0)
-        nc.scalar.dma_start(out=b_row[0:1, :], in_=b_out.rearrange("(o d) -> o d", o=1))
         w_raw = const.tile([P, PASSES, 4 * D], BF16)
-        nc.sync.dma_start(
-            out=w_raw[:],
-            in_=w_out.rearrange("(c q t) n -> q c (t n)", c=PASSES, t=4),
-        )
-
+        w_passes = w_out.rearrange("(c q t) n -> c q (t n)", c=PASSES, t=4)
         u_sb, a_sb, x_sb = [], [], []
         for j in range(PAIRS):
+            if j < PASSES:
+                nc.sync.dma_start(out=w_raw[:, j, :], in_=w_passes[j])
             u_j = inputs.tile([P, PAIR * D], BF16, name="u%d" % j)
             a_j = inputs.tile([P, PAIR * D], BF16, name="a%d" % j)
             x_j = inputs.tile([P, PAIR * D], BF16, name="x%d" % j)
@@ -91,35 +88,29 @@ def tile_stulayer_pb_t_kernel(tc, u, attn_out, src_norm, w_out, b_out, ln2_w, ln
         vec_cols = const.tile([P, 2 * BLOCKS], F32)
         b_bc = const.tile([P, D], F32)
 
-        def regroup_weight():
-            for c in range(PASSES):
-                rows_of_pass = w_raw[:, c, :].rearrange("p (t n) -> p n t", t=4)
-                words_of_pass = w_grouped[:, c, :].rearrange("p (n t) -> p n t", t=4)
-                if c == 0:
-                    nc.vector.tensor_copy(out=words_of_pass, in_=rows_of_pass)
-                else:
-                    nc.scalar.copy(out=words_of_pass, in_=rows_of_pass)
+        def regroup_weight(c, copy, half):
+            cols = slice(half * D // 2, (half + 1) * D // 2)
+            copy(
+                out=w_grouped[:, c, :].rearrange("p (n t) -> p n t", t=4)[:, cols, :],
+                in_=w_raw[:, c, :].rearrange("p (t n) -> p n t", t=4)[:, cols, :],
+            )
 
-        def quantise_weight():
-            for c in range(PASSES):
-                nc.vector.quantize_mx(
-                    out=w_codes[:, c, :].bitcast(FP8X4), scales=w_scales[:, c, :], in_=w_grouped[:, c, :]
-                )
+        def quantise_weight(c):
+            nc.vector.quantize_mx(
+                out=w_codes[:, c, :].bitcast(FP8X4), scales=w_scales[:, c, :], in_=w_grouped[:, c, :]
+            )
 
         def prepare_gain_shift():
-            nc.vector.tensor_copy(out=vec_rows_f32[:], in_=vec_rows[:])
             vec_t = psum.tile([P, D], F32, tag="w_ps")
             nc.tensor.transpose(vec_t[:, 0:P], vec_rows_f32[:], ident[:])
-            nc.vector.tensor_copy(out=vec_cols[:], in_=vec_t[:, 0 : 2 * BLOCKS])
+            nc.scalar.copy(out=vec_cols[:], in_=vec_t[:, 0 : 2 * BLOCKS])
 
         def prepare_bias():
             b_ps = psum.tile([P, D], F32, tag="y_t")
             nc.tensor.matmul(out=b_ps[:], lhsT=ones[:], rhs=b_row[:], start=True, stop=True)
-            nc.vector.tensor_scalar(
-                out=b_bc[:], in0=b_ps[:], scalar1=1.0 / D, scalar2=0.0, op0=ALU.mult, op1=ALU.add
-            )
+            nc.scalar.activation(out=b_bc[:], in_=b_ps[:], func=ACT.Copy, scale=1.0 / D)
 
-        res, cat_t, grouped, codes, scales, z, zb, y, y_t, w_t, w_ps, result = {}, {}, {}, {}, {}, {}, {}, {}, {}, {}, {}, {}
+        res, src, cat_t, grouped, codes, scales, z, zb, y, y_t, w_t, w_ps, result = {}, {}, {}, {}, {}, {}, {}, {}, {}, {}, {}, {}, {}
         mean, neg_mean, sq_sum, rstd = {}, {}, {}, {}
 
         def add_inputs(m):
@@ -128,15 +119,19 @@ def tile_stulayer_pb_t_kernel(tc, u, attn_out, src_norm, w_out, b_out, ln2_w, ln
             res[m] = three.tile([P, D], BF16, name="res")
             nc.vector.tensor_tensor(out=res[m][:], in0=u_sb[j][:, cols], in1=a_sb[j][:, cols], op=ALU.add)
 
-        def transpose_cat(m):
+        def split_src(m):
             j, i = divmod(m, PAIR)
-            cat_words = [res[m][:].bitcast(F32), x_sb[j][:].bitcast(F32)[:, i * (D // 2) : (i + 1) * (D // 2)]]
+            src_words = x_sb[j][:].bitcast(U32)[:, i * (D // 2) : (i + 1) * (D // 2)]
+            src[m] = three.tile([P, HALVES, P], U32, name="src")
+            nc.gpsimd.tensor_copy(out=src[m][:], in_=src_words.rearrange("p (q h) -> p h q", h=HALVES))
+
+        def transpose_cat(m):
+            res_words = res[m][:].bitcast(F32)
             cat_t[m] = psum.tile([P, PASSES * HALVES, P], F32, tag="cat_t", name="cat_t")
-            for c in range(PASSES):
-                for h in range(HALVES):
-                    nc.tensor.transpose(
-                        cat_t[m][:, c * HALVES + h, :], cat_words[c][:, h : HALVES * P : HALVES], ident[:]
-                    )
+            for h in range(HALVES):
+                nc.tensor.transpose(cat_t[m][:, h, :], res_words[:, h : HALVES * P : HALVES], ident[:])
+            for h in range(HALVES):
+                nc.tensor.transpose(cat_t[m][:, HALVES + h, :], src[m][:, h, :].bitcast(F32), ident[:])
 
         def copy_cat(m):
             grouped[m] = seven.tile([P, PASSES * P * 4], BF16, align_bytes=64, name="grouped")
@@ -242,6 +237,7 @@ def tile_stulayer_pb_t_kernel(tc, u, attn_out, src_norm, w_out, b_out, ln2_w, ln
             run(add_inputs, h)
             run(quantise, h - QUANT_LAG)
             run(normalise, h - NORM_LAG)
+            run(split_src, h)
             run(add_bias, h - 5)
             run(mean_over_d, h - 5)
             run(add_src, h - 13)
@@ -255,11 +251,19 @@ def tile_stulayer_pb_t_kernel(tc, u, attn_out, src_norm, w_out, b_out, ln2_w, ln
             run(project, h - 4)
 
         with tc.manual_schedule():
-            regroup_weight()
-            for h in range(ROUNDS_BEFORE_QUANTISING_WEIGHT):
-                one_round(h)
-            quantise_weight()
+            regroup_weight(0, nc.vector.tensor_copy, 0)
+            regroup_weight(0, nc.scalar.copy, 1)
             prepare_bias()
+            one_round(0)
+            one_round(1)
+            regroup_weight(1, nc.vector.tensor_copy, 0)
+            quantise_weight(0)
+            one_round(2)
+            regroup_weight(1, nc.scalar.copy, 1)
+            one_round(3)
+            quantise_weight(1)
+            nc.vector.tensor_copy(out=vec_rows_f32[:], in_=vec_rows[:])
+            one_round(4)
             prepare_gain_shift()
-            for h in range(ROUNDS_BEFORE_QUANTISING_WEIGHT, TILES + LAST_LAG + 1):
+            for h in range(5, TILES + LAST_LAG + 1):
                 one_round(h)

@@ -24,6 +24,7 @@ PAIRS = ROWS // PAIR_ROWS
 EPS = 1e-5
 QUANT_LAG = 3
 NORM_LAG = 7
+PAIRS_AHEAD = 6
 LAST_LAG = 13
 
 FLOPS = 2 * ROWS * (PASSES * 512) * D
@@ -59,18 +60,17 @@ def tile_stulayer_pb_t_kernel(tc, u, attn_out, src_norm, w_out, b_out, ln2_w, ln
         w_raw = const.tile([P, PASSES, 4 * D], BF16)
         w_passes = w_out.rearrange("(c q t) n -> c q (t n)", c=PASSES, t=4)
         u_sb, a_sb, x_sb = [], [], []
-        for j in range(PAIRS):
+
+        def load_pair(j):
             if j < PASSES:
                 nc.sync.dma_start(out=w_raw[:, j, :], in_=w_passes[j])
-            u_j = inputs.tile([P, PAIR * D], BF16, name="u%d" % j)
-            a_j = inputs.tile([P, PAIR * D], BF16, name="a%d" % j)
-            x_j = inputs.tile([P, PAIR * D], BF16, name="x%d" % j)
-            nc.sync.dma_start(out=u_j[:], in_=pair_rows(u, j))
-            nc.sync.dma_start(out=a_j[:], in_=pair_rows(attn_out, j))
-            nc.sync.dma_start(out=x_j[:], in_=pair_rows(src_norm, j))
-            u_sb.append(u_j)
-            a_sb.append(a_j)
-            x_sb.append(x_j)
+            for x, tiles, name in ((u, u_sb, "u"), (attn_out, a_sb, "a"), (src_norm, x_sb, "x")):
+                x_j = inputs.tile([P, PAIR * D], BF16, name="%s%d" % (name, j))
+                nc.sync.dma_start(out=x_j[:], in_=pair_rows(x, j))
+                tiles.append(x_j)
+
+        for j in range(PAIRS_AHEAD):
+            load_pair(j)
 
         ident = const.tile([P, P], F32)
         make_identity(nc, ident[:])
@@ -110,7 +110,7 @@ def tile_stulayer_pb_t_kernel(tc, u, attn_out, src_norm, w_out, b_out, ln2_w, ln
             nc.tensor.matmul(out=b_ps[:], lhsT=ones[:], rhs=b_row[:], start=True, stop=True)
             nc.scalar.activation(out=b_bc[:], in_=b_ps[:], func=ACT.Copy, scale=1.0 / D)
 
-        res, src, cat_t, grouped, codes, scales, z, zb, y, y_t, w_t, w_ps, result = {}, {}, {}, {}, {}, {}, {}, {}, {}, {}, {}, {}, {}
+        res, cat_t, grouped, codes, scales, z, zb, y, y_t, w_t, w_ps, result = {}, {}, {}, {}, {}, {}, {}, {}, {}, {}, {}, {}
         mean, neg_mean, sq_sum, rstd = {}, {}, {}, {}
 
         def add_inputs(m):
@@ -119,19 +119,15 @@ def tile_stulayer_pb_t_kernel(tc, u, attn_out, src_norm, w_out, b_out, ln2_w, ln
             res[m] = three.tile([P, D], BF16, name="res")
             nc.vector.tensor_tensor(out=res[m][:], in0=u_sb[j][:, cols], in1=a_sb[j][:, cols], op=ALU.add)
 
-        def split_src(m):
-            j, i = divmod(m, PAIR)
-            src_words = x_sb[j][:].bitcast(U32)[:, i * (D // 2) : (i + 1) * (D // 2)]
-            src[m] = three.tile([P, HALVES, P], U32, name="src")
-            nc.gpsimd.tensor_copy(out=src[m][:], in_=src_words.rearrange("p (q h) -> p h q", h=HALVES))
-
         def transpose_cat(m):
-            res_words = res[m][:].bitcast(F32)
+            j, i = divmod(m, PAIR)
+            cat_words = [res[m][:].bitcast(F32), x_sb[j][:].bitcast(F32)[:, i * (D // 2) : (i + 1) * (D // 2)]]
             cat_t[m] = psum.tile([P, PASSES * HALVES, P], F32, tag="cat_t", name="cat_t")
-            for h in range(HALVES):
-                nc.tensor.transpose(cat_t[m][:, h, :], res_words[:, h : HALVES * P : HALVES], ident[:])
-            for h in range(HALVES):
-                nc.tensor.transpose(cat_t[m][:, HALVES + h, :], src[m][:, h, :].bitcast(F32), ident[:])
+            for c in range(PASSES):
+                for h in range(HALVES):
+                    nc.tensor.transpose(
+                        cat_t[m][:, c * HALVES + h, :], cat_words[c][:, h : HALVES * P : HALVES], ident[:]
+                    )
 
         def copy_cat(m):
             grouped[m] = seven.tile([P, PASSES * P * 4], BF16, align_bytes=64, name="grouped")
@@ -234,10 +230,11 @@ def tile_stulayer_pb_t_kernel(tc, u, attn_out, src_norm, w_out, b_out, ln2_w, ln
                 stage(m)
 
         def one_round(h):
+            if h % PAIR == 0 and PAIRS_AHEAD <= h // PAIR + PAIRS_AHEAD < PAIRS:
+                load_pair(h // PAIR + PAIRS_AHEAD)
             run(add_inputs, h)
             run(quantise, h - QUANT_LAG)
             run(normalise, h - NORM_LAG)
-            run(split_src, h)
             run(add_bias, h - 5)
             run(mean_over_d, h - 5)
             run(add_src, h - 13)

@@ -24,8 +24,12 @@ PAIRS = ROWS // PAIR_ROWS
 EPS = 1e-5
 QUANT_LAG = 3
 NORM_LAG = 7
+ROW_WAY = TILES - PAIR
+SPREAD_ROUND = 22
 PAIRS_AHEAD = 6
-LAST_LAG = 13
+Y_LAG = 9
+BACK_LAG = 11
+LAST_LAG = 11
 
 FLOPS = 2 * ROWS * (PASSES * 512) * D
 
@@ -69,7 +73,7 @@ def tile_stulayer_pb_t_kernel(tc, u, attn_out, src_norm, w_out, b_out, ln2_w, ln
                 nc.sync.dma_start(out=x_j[:], in_=pair_rows(x, j))
                 tiles.append(x_j)
 
-        for j in range(PAIRS_AHEAD):
+        for j in range(PAIRS_AHEAD + 2):
             load_pair(j)
 
         ident = const.tile([P, P], F32)
@@ -87,6 +91,8 @@ def tile_stulayer_pb_t_kernel(tc, u, attn_out, src_norm, w_out, b_out, ln2_w, ln
         vec_rows_f32 = const.tile([P, P], F32)
         vec_cols = const.tile([P, 2 * BLOCKS], F32)
         b_bc = const.tile([P, D], F32)
+        gain_bc = const.tile([P, D], BF16)
+        shift_bc = const.tile([P, D], BF16)
 
         def regroup_weight(c, copy, half):
             cols = slice(half * D // 2, (half + 1) * D // 2)
@@ -112,6 +118,7 @@ def tile_stulayer_pb_t_kernel(tc, u, attn_out, src_norm, w_out, b_out, ln2_w, ln
 
         res, cat_t, grouped, codes, scales, z, zb, y, y_t, w_t, w_ps, result = {}, {}, {}, {}, {}, {}, {}, {}, {}, {}, {}, {}
         mean, neg_mean, sq_sum, rstd = {}, {}, {}, {}
+        shifted, centred = {}, {}
 
         def add_inputs(m):
             j, i = divmod(m, PAIR)
@@ -191,12 +198,33 @@ def tile_stulayer_pb_t_kernel(tc, u, attn_out, src_norm, w_out, b_out, ln2_w, ln
                 out=y[m], in0=zb[m][:], scalar1=neg_mean[m][:], scalar2=rstd[m][:], op0=ALU.add, op1=ALU.mult
             )
 
+        def add_shift(m):
+            j, i = divmod(m, PAIR)
+            shifted[m] = two.tile([P, D], F32, name="shifted")
+            nc.vector.tensor_tensor(
+                out=shifted[m][:], in0=x_sb[j][:, i * D : (i + 1) * D], in1=shift_bc[:], op=ALU.add
+            )
+
+        def centre_gain(m):
+            centred[m] = two.tile([P, D], F32, name="centred")
+            nc.vector.scalar_tensor_tensor(
+                out=centred[m][:], in0=zb[m][:], scalar=neg_mean[m][:], in1=gain_bc[:], op0=ALU.add, op1=ALU.mult
+            )
+
+        def finish_row(m):
+            result[m] = four.tile([P, D], F32, name="result")
+            nc.vector.scalar_tensor_tensor(
+                out=result[m][:], in0=centred[m][:], scalar=rstd[m][:], in1=shifted[m][:], op0=ALU.mult, op1=ALU.add
+            )
+            nc.sync.dma_start(out=tile_rows(out, m), in_=result[m][:])
+
         def blocks_of(bank):
             return range(bank * (BLOCKS // PAIR), (bank + 1) * (BLOCKS // PAIR))
 
         def transpose_y(s):
             j, bank = divmod(s, PAIR)
-            y_t[s] = psum.tile([P, BLOCKS // PAIR, PAIR, P], F32, tag="y_t", name="y_t")
+            tag = "cat_t" if s % 2 and s + Y_LAG > TILES + 1 else "y_t"
+            y_t[s] = psum.tile([P, BLOCKS // PAIR, PAIR, P], F32, tag=tag, name="y_t")
             for slot, f in enumerate(blocks_of(bank)):
                 for i in range(PAIR):
                     nc.tensor.transpose(y_t[s][:, slot, i, :], y[j * PAIR + i][:, f * P : (f + 1) * P], ident[:])
@@ -213,7 +241,8 @@ def tile_stulayer_pb_t_kernel(tc, u, attn_out, src_norm, w_out, b_out, ln2_w, ln
 
         def transpose_back(m):
             j, i = divmod(m, PAIR)
-            w_ps[m] = psum.tile([P, D], F32, tag="w_ps", name="w_ps")
+            tag = "z" if m % 2 and m + BACK_LAG > TILES + 4 else "w_ps"
+            w_ps[m] = psum.tile([P, D], F32, tag=tag, name="w_ps")
             for f in range(BLOCKS):
                 nc.tensor.transpose(w_ps[m][:, f * P : (f + 1) * P], w_t[j][:, f, i, :], ident[:])
 
@@ -225,42 +254,58 @@ def tile_stulayer_pb_t_kernel(tc, u, attn_out, src_norm, w_out, b_out, ln2_w, ln
             )
             nc.sync.dma_start(out=tile_rows(out, m), in_=result[m][:])
 
-        def run(stage, m):
-            if 0 <= m < TILES:
+        def run(stage, m, first=0, end=TILES):
+            if first <= m < end:
                 stage(m)
 
         def one_round(h):
-            if h % PAIR == 0 and PAIRS_AHEAD <= h // PAIR + PAIRS_AHEAD < PAIRS:
+            if h % PAIR == 0 and h // PAIR + PAIRS_AHEAD < PAIRS:
                 load_pair(h // PAIR + PAIRS_AHEAD)
+            if h == SPREAD_ROUND:
+                nc.sync.dma_start(out=gain_bc[:], in_=ln2_w.partition_broadcast(P))
+                nc.sync.dma_start(out=shift_bc[:], in_=ln2_b.partition_broadcast(P))
+            run(transpose_y, h - Y_LAG, end=ROW_WAY)
+            run(transpose_back, h - BACK_LAG, end=ROW_WAY)
             run(add_inputs, h)
+            run(add_shift, h - 2, first=ROW_WAY)
             run(quantise, h - QUANT_LAG)
-            run(normalise, h - NORM_LAG)
+            run(normalise, h - NORM_LAG, end=ROW_WAY)
             run(add_bias, h - 5)
             run(mean_over_d, h - 5)
-            run(add_src, h - 13)
+            run(add_src, h - 11, end=ROW_WAY)
+            run(centre_gain, h - 6, first=ROW_WAY)
+            run(finish_row, h - 7, first=ROW_WAY)
             run(copy_cat, h - 2)
             run(square_sum, h - 6)
-            run(gain_shift, h - 10)
+            run(gain_shift, h - 9, end=ROW_WAY)
             run(inverse_deviation, h - 6)
-            run(transpose_back, h - 12)
-            run(transpose_y, h - 9)
             run(transpose_cat, h - 1)
             run(project, h - 4)
 
         with tc.manual_schedule():
             regroup_weight(0, nc.vector.tensor_copy, 0)
             regroup_weight(0, nc.scalar.copy, 1)
-            prepare_bias()
-            one_round(0)
-            one_round(1)
+            for m in range(PAIR):
+                add_inputs(m)
+                transpose_cat(m)
+            copy_cat(0)
             regroup_weight(1, nc.vector.tensor_copy, 0)
-            quantise_weight(0)
-            one_round(2)
             regroup_weight(1, nc.scalar.copy, 1)
-            one_round(3)
+            prepare_bias()
+            quantise_weight(0)
+            quantise(0)
             quantise_weight(1)
+            project(0)
+            copy_cat(1)
             nc.vector.tensor_copy(out=vec_rows_f32[:], in_=vec_rows[:])
-            one_round(4)
             prepare_gain_shift()
+            add_inputs(2)
+            add_inputs(3)
+            transpose_cat(2)
+            load_pair(PAIRS_AHEAD + 2)
+            add_inputs(4)
+            quantise(1)
+            copy_cat(2)
+            transpose_cat(3)
             for h in range(5, TILES + LAST_LAG + 1):
                 one_round(h)

from contextlib import ExitStack

import concourse.mybir as mybir
from concourse.masks import make_identity

F32 = mybir.dt.float32
BF16 = mybir.dt.bfloat16
U32 = mybir.dt.uint32
U8 = mybir.dt.uint8
FP8X4 = mybir.dt.float8_e4m3fn_x4
ALU = mybir.AluOpType
ACT = mybir.ActivationFunctionType

P = 128
ROWS = 512 * 8
D = 512
BLOCKS = D // P
PASSES = 2
HALVES = 2
TILES = ROWS // P
PAIR = 2
PAIR_ROWS = PAIR * P
PAIRS = ROWS // PAIR_ROWS
EPS = 1e-5
QUANT_LAG = 3
NORM_LAG = 7
ROW_WAY = TILES - PAIR
SPREAD_ROUND = 22
PAIRS_AHEAD = 6
Y_LAG = 9
BACK_LAG = 11
LAST_LAG = 11

FLOPS = 2 * ROWS * (PASSES * 512) * D


def tile_stulayer_pb_t_kernel(tc, u, attn_out, src_norm, w_out, b_out, ln2_w, ln2_b, out):
    nc = tc.nc

    def pair_rows(x, j):
        rows = x.flatten_outer_dims()[j * PAIR_ROWS : (j + 1) * PAIR_ROWS, :]
        return rows.rearrange("(p i) d -> p (i d)", i=PAIR)

    def tile_rows(x, m):
        j, i = divmod(m, PAIR)
        return pair_rows(x, j)[:, i * D : (i + 1) * D]

    with ExitStack() as pools:
        const = pools.enter_context(tc.tile_pool(name="const", bufs=1))
        inputs = pools.enter_context(tc.tile_pool(name="inputs", bufs=1))
        two = pools.enter_context(tc.tile_pool(name="two", bufs=2))
        three = pools.enter_context(tc.tile_pool(name="three", bufs=3))
        four = pools.enter_context(tc.tile_pool(name="four", bufs=4))
        seven = pools.enter_context(tc.tile_pool(name="seven", bufs=7))
        psum = pools.enter_context(tc.psum_pool(name="psum", bufs=2))

        b_row = const.tile([P, D], BF16)
        nc.vector.memset(b_row[:], 0.0)
        nc.scalar.dma_start(out=b_row[0:1, :], in_=b_out.rearrange("(o d) -> o d", o=1))
        vec_rows = const.tile([P, P], BF16)
        nc.vector.memset(vec_rows[:], 0.0)
        nc.scalar.dma_start(out=vec_rows[0:BLOCKS, :], in_=ln2_w.rearrange("(f p) -> f p", p=P))
        nc.scalar.dma_start(out=vec_rows[BLOCKS : 2 * BLOCKS, :], in_=ln2_b.rearrange("(f p) -> f p", p=P))
        w_raw = const.tile([P, PASSES, 4 * D], BF16)
        w_passes = w_out.rearrange("(c q t) n -> c q (t n)", c=PASSES, t=4)
        u_sb, a_sb, x_sb = [], [], []

        def load_pair(j):
            if j < PASSES:
                nc.sync.dma_start(out=w_raw[:, j, :], in_=w_passes[j])
            for x, tiles, name in ((u, u_sb, "u"), (attn_out, a_sb, "a"), (src_norm, x_sb, "x")):
                x_j = inputs.tile([P, PAIR * D], BF16, name="%s%d" % (name, j))
                nc.sync.dma_start(out=x_j[:], in_=pair_rows(x, j))
                tiles.append(x_j)

        for j in range(PAIRS_AHEAD + 2):
            load_pair(j)

        ident = const.tile([P, P], F32)
        make_identity(nc, ident[:])
        ones = const.tile([P, P], BF16)
        nc.vector.memset(ones[:], 1.0)
        eps_col = const.tile([P, 1], F32)
        nc.vector.memset(eps_col[:], EPS / D**2)
        first_rsqrt = const.tile([P, 1], F32)
        nc.scalar.activation(out=first_rsqrt[:], in_=eps_col[:], func=ACT.Abs_reciprocal_sqrt)

        w_grouped = const.tile([P, PASSES, D * 4], BF16, align_bytes=64)
        w_codes = const.tile([P, PASSES, D], U32, align_bytes=64)
        w_scales = const.tile([P, PASSES, D], U8, align_bytes=64)
        vec_rows_f32 = const.tile([P, P], F32)
        vec_cols = const.tile([P, 2 * BLOCKS], F32)
        b_bc = const.tile([P, D], F32)
        gain_bc = const.tile([P, D], BF16)
        shift_bc = const.tile([P, D], BF16)

        def regroup_weight(c, copy, half):
            cols = slice(half * D // 2, (half + 1) * D // 2)
            copy(
                out=w_grouped[:, c, :].rearrange("p (n t) -> p n t", t=4)[:, cols, :],
                in_=w_raw[:, c, :].rearrange("p (t n) -> p n t", t=4)[:, cols, :],
            )

        def quantise_weight(c):
            nc.vector.quantize_mx(
                out=w_codes[:, c, :].bitcast(FP8X4), scales=w_scales[:, c, :], in_=w_grouped[:, c, :]
            )

        def prepare_gain_shift():
            vec_t = psum.tile([P, D], F32, tag="w_ps")
            nc.tensor.transpose(vec_t[:, 0:P], vec_rows_f32[:], ident[:])
            nc.scalar.copy(out=vec_cols[:], in_=vec_t[:, 0 : 2 * BLOCKS])

        def prepare_bias():
            b_ps = psum.tile([P, D], F32, tag="y_t")
            nc.tensor.matmul(out=b_ps[:], lhsT=ones[:], rhs=b_row[:], start=True, stop=True)
            nc.scalar.activation(out=b_bc[:], in_=b_ps[:], func=ACT.Copy, scale=1.0 / D)

        res, cat_t, grouped, codes, scales, z, zb, y, y_t, w_t, w_ps, result = {}, {}, {}, {}, {}, {}, {}, {}, {}, {}, {}, {}
        mean, neg_mean, sq_sum, rstd = {}, {}, {}, {}
        shifted, centred = {}, {}

        def add_inputs(m):
            j, i = divmod(m, PAIR)
            cols = slice(i * D, (i + 1) * D)
            res[m] = three.tile([P, D], BF16, name="res")
            nc.vector.tensor_tensor(out=res[m][:], in0=u_sb[j][:, cols], in1=a_sb[j][:, cols], op=ALU.add)

        def transpose_cat(m):
            j, i = divmod(m, PAIR)
            cat_words = [res[m][:].bitcast(F32), x_sb[j][:].bitcast(F32)[:, i * (D // 2) : (i + 1) * (D // 2)]]
            cat_t[m] = psum.tile([P, PASSES * HALVES, P], F32, tag="cat_t", name="cat_t")
            for c in range(PASSES):
                for h in range(HALVES):
                    nc.tensor.transpose(
                        cat_t[m][:, c * HALVES + h, :], cat_words[c][:, h : HALVES * P : HALVES], ident[:]
                    )

        def copy_cat(m):
            grouped[m] = seven.tile([P, PASSES * P * 4], BF16, align_bytes=64, name="grouped")
            nc.scalar.copy(
                out=grouped[m][:].bitcast(F32).rearrange("p (c r h) -> p c r h", c=PASSES, h=HALVES),
                in_=cat_t[m][:].rearrange("p (c h) r -> p c r h", h=HALVES),
            )

        def quantise(m):
            codes[m] = three.tile([P, PASSES * P], U32, align_bytes=64, name="codes")
            scales[m] = three.tile([P, PASSES * P], U8, align_bytes=64, name="scales")
            nc.vector.quantize_mx(out=codes[m][:].bitcast(FP8X4), scales=scales[m][:], in_=grouped[m][:])

        def project(m):
            z[m] = psum.tile([P, D], F32, tag="z", name="z")
            for c in range(PASSES):
                cols = slice(c * P, (c + 1) * P)
                nc.tensor.matmul_mx(
                    out=z[m][:],
                    lhsT=codes[m][:, cols].bitcast(FP8X4),
                    lhsT_scale=scales[m][:, cols],
                    rhs=w_codes[:, c, :].bitcast(FP8X4),
                    rhs_scale=w_scales[:, c, :],
                    start=(c == 0),
                    stop=(c == PASSES - 1),
                )

        def add_bias(m):
            zb[m] = four.tile([P, D], F32, name="zb")
            mean[m] = four.tile([P, 1], F32, name="mean")
            nc.vector.scalar_tensor_tensor(
                out=zb[m][:], in0=z[m][:], scalar=1.0 / D, in1=b_bc[:], op0=ALU.mult, op1=ALU.add,
                accum_out=mean[m][:],
            )

        def mean_over_d(m):
            neg_mean[m] = four.tile([P, 1], F32, name="neg_mean")
            nc.gpsimd.tensor_scalar(
                out=neg_mean[m][:], in0=mean[m][:], scalar1=-1.0 / D, scalar2=0.0, op0=ALU.mult, op1=ALU.add
            )

        def square_sum(m):
            squares = two.tile([P, D], BF16, name="squares")
            sq_sum[m] = four.tile([P, 1], F32, name="sq_sum")
            nc.scalar.activation(
                out=squares[:], in_=zb[m][:], func=ACT.Square, bias=mean[m][:], scale=float(-D),
                accum_out=sq_sum[m][:],
            )

        def inverse_deviation(m):
            rstd[m] = four.tile([P, 1], F32, name="rstd")
            nc.scalar.activation(
                out=rstd[m][:], in_=sq_sum[m][:], func=ACT.Abs_reciprocal_sqrt, bias=eps_col[:], scale=1.0 / D**3
            )

        def normalise(m):
            k = m + NORM_LAG - QUANT_LAG
            y_tile = grouped[k] if k < TILES else seven.tile([P, PASSES * P * 4], BF16, align_bytes=64, name="grouped")
            y[m] = y_tile[:].bitcast(F32)
            nc.gpsimd.tensor_scalar(
                out=y[m], in0=zb[m][:], scalar1=neg_mean[m][:], scalar2=rstd[m][:], op0=ALU.add, op1=ALU.mult
            )

        def add_shift(m):
            j, i = divmod(m, PAIR)
            shifted[m] = two.tile([P, D], F32, name="shifted")
            nc.vector.tensor_tensor(
                out=shifted[m][:], in0=x_sb[j][:, i * D : (i + 1) * D], in1=shift_bc[:], op=ALU.add
            )

        def centre_gain(m):
            centred[m] = two.tile([P, D], F32, name="centred")
            nc.vector.scalar_tensor_tensor(
                out=centred[m][:], in0=zb[m][:], scalar=neg_mean[m][:], in1=gain_bc[:], op0=ALU.add, op1=ALU.mult
            )

        def finish_row(m):
            result[m] = four.tile([P, D], F32, name="result")
            nc.vector.scalar_tensor_tensor(
                out=result[m][:], in0=centred[m][:], scalar=rstd[m][:], in1=shifted[m][:], op0=ALU.mult, op1=ALU.add
            )
            nc.sync.dma_start(out=tile_rows(out, m), in_=result[m][:])

        def blocks_of(bank):
            return range(bank * (BLOCKS // PAIR), (bank + 1) * (BLOCKS // PAIR))

        def transpose_y(s):
            j, bank = divmod(s, PAIR)
            tag = "cat_t" if s % 2 and s + Y_LAG > TILES + 1 else "y_t"
            y_t[s] = psum.tile([P, BLOCKS // PAIR, PAIR, P], F32, tag=tag, name="y_t")
            for slot, f in enumerate(blocks_of(bank)):
                for i in range(PAIR):
                    nc.tensor.transpose(y_t[s][:, slot, i, :], y[j * PAIR + i][:, f * P : (f + 1) * P], ident[:])

        def gain_shift(s):
            j, bank = divmod(s, PAIR)
            if bank == 0:
                w_t[j] = three.tile([P, BLOCKS, PAIR, P], F32, name="w_t")
            for slot, f in enumerate(blocks_of(bank)):
                nc.scalar.activation(
                    out=w_t[j][:, f, :, :], in_=y_t[s][:, slot, :, :], func=ACT.Identity,
                    scale=vec_cols[:, f : f + 1], bias=vec_cols[:, BLOCKS + f : BLOCKS + f + 1],
                )

        def transpose_back(m):
            j, i = divmod(m, PAIR)
            tag = "z" if m % 2 and m + BACK_LAG > TILES + 4 else "w_ps"
            w_ps[m] = psum.tile([P, D], F32, tag=tag, name="w_ps")
            for f in range(BLOCKS):
                nc.tensor.transpose(w_ps[m][:, f * P : (f + 1) * P], w_t[j][:, f, i, :], ident[:])

        def add_src(m):
            j, i = divmod(m, PAIR)
            result[m] = four.tile([P, D], F32, name="result")
            nc.vector.tensor_tensor(
                out=result[m][:], in0=w_ps[m][:], in1=x_sb[j][:, i * D : (i + 1) * D], op=ALU.add
            )
            nc.sync.dma_start(out=tile_rows(out, m), in_=result[m][:])

        def run(stage, m, first=0, end=TILES):
            if first <= m < end:
                stage(m)

        def one_round(h):
            if h % PAIR == 0 and h // PAIR + PAIRS_AHEAD < PAIRS:
                load_pair(h // PAIR + PAIRS_AHEAD)
            if h == SPREAD_ROUND:
                nc.sync.dma_start(out=gain_bc[:], in_=ln2_w.partition_broadcast(P))
                nc.sync.dma_start(out=shift_bc[:], in_=ln2_b.partition_broadcast(P))
            run(transpose_y, h - Y_LAG, end=ROW_WAY)
            run(transpose_back, h - BACK_LAG, end=ROW_WAY)
            run(add_inputs, h)
            run(add_shift, h - 2, first=ROW_WAY)
            run(quantise, h - QUANT_LAG)
            run(normalise, h - NORM_LAG, end=ROW_WAY)
            run(add_bias, h - 5)
            run(mean_over_d, h - 5)
            run(add_src, h - 11, end=ROW_WAY)
            run(centre_gain, h - 6, first=ROW_WAY)
            run(finish_row, h - 7, first=ROW_WAY)
            run(copy_cat, h - 2)
            run(square_sum, h - 6)
            run(gain_shift, h - 9, end=ROW_WAY)
            run(inverse_deviation, h - 6)
            run(transpose_cat, h - 1)
            run(project, h - 4)

        with tc.manual_schedule():
            regroup_weight(0, nc.vector.tensor_copy, 0)
            regroup_weight(0, nc.scalar.copy, 1)
            for m in range(PAIR):
                add_inputs(m)
                transpose_cat(m)
            copy_cat(0)
            regroup_weight(1, nc.vector.tensor_copy, 0)
            regroup_weight(1, nc.scalar.copy, 1)
            prepare_bias()
            quantise_weight(0)
            quantise(0)
            quantise_weight(1)
            project(0)
            copy_cat(1)
            nc.vector.tensor_copy(out=vec_rows_f32[:], in_=vec_rows[:])
            prepare_gain_shift()
            add_inputs(2)
            add_inputs(3)
            transpose_cat(2)
            load_pair(PAIRS_AHEAD + 2)
            add_inputs(4)
            quantise(1)
            copy_cat(2)
            transpose_cat(3)
            for h in range(5, TILES + LAST_LAG + 1):
                one_round(h)
